import numpy as np
import ml_dtypes


def mxq(x, axis, fmt="e4m3"):
    dtype, down = {"e4m3": (ml_dtypes.float8_e4m3fn, 7), "e5m2": (ml_dtypes.float8_e5m2, 14)}[fmt]
    v = np.moveaxis(np.asarray(x, np.float32).astype(ml_dtypes.bfloat16).astype(np.float64), axis, -1)
    blocks = v.reshape(v.shape[:-1] + (-1, 32))
    amax = np.abs(blocks).max(-1, keepdims=True)
    byte = np.maximum(np.where(amax > 0, np.frexp(amax)[1] - 1 + 127, 0) - down, 1)
    scale = np.exp2(byte - 127.0)
    codes = (blocks / scale).astype(np.float32).astype(dtype).astype(np.float64)
    return np.moveaxis((codes * scale).reshape(v.shape), -1, axis)


WIDE = False


def mx_kscale(k):
    if not WIDE:
        return np.ones(k)
    levels = np.array([10, -10, 5, -5, 0])
    a = np.random.permutation(np.resize(levels, k // 512 * 4)).reshape(k // 512, 4)
    idx = np.arange(k)
    return np.exp2(a[idx // 512, idx % 128 // 32])


BF16 = ml_dtypes.bfloat16


def bf(x):
    return np.asarray(x, np.float32).astype(BF16)


def f64(x):
    return np.asarray(x).astype(np.float64)


B, C, D, DV, H, W = 2, 1024, 128, 256, 64, 64
N = H * W
HP, WP = H // 2, W // 2
M = HP * WP


def maxpool2(t):
    return t.reshape(B, t.shape[1], HP, 2, WP, 2).max(axis=(3, 5))


def setup_inputs():
    s = mx_kscale(C)
    return {"x": bf(np.random.standard_normal((B, C, H, W)) * s[None, :, None, None]),
            "Wq": bf(np.random.standard_normal((D, C)) * 0.5 / np.sqrt(C) / s[None, :]),
            "Wk": bf(np.random.standard_normal((D, C)) * 0.5 / np.sqrt(C) / s[None, :]),
            "Wv": bf(np.random.standard_normal((DV, C)) / np.sqrt(C) / s[None, :])}


def reference(x, Wq, Wk, Wv):
    xq = mxq(f64(x).reshape(B, C, N), 1, "e4m3")
    q = (mxq(f64(Wq), 1, "e4m3") @ xq).transpose(0, 2, 1)
    k = maxpool2((mxq(f64(Wk), 1, "e4m3") @ xq).reshape(B, D, H, W)).reshape(B, D, M)
    v = maxpool2((mxq(f64(Wv), 1, "e4m3") @ xq).reshape(B, DV, H, W)).reshape(B, DV, M)
    return q, k, v

@@ -1,0 +1,201 @@
+from contextlib import ExitStack
+
+import concourse.mybir as mybir
+from concourse.masks import make_identity
+
+F32 = mybir.dt.float32
+BF16 = mybir.dt.bfloat16
+U32 = mybir.dt.uint32
+U8 = mybir.dt.uint8
+FP8X4 = mybir.dt.float8_e4m3fn_x4
+
+P = 128
+PACK = 4
+K_PASS = P * PACK
+
+BATCH, CHANNELS, HEIGHT, WIDTH = 2, 1024, 64, 64
+POSITIONS = HEIGHT * WIDTH
+PASSES = CHANNELS // K_PASS
+Q_CHANNELS = 128
+WEIGHT_TILES = 4
+POOLED_TILES = 3
+
+CHUNK = 512
+CHUNKS = BATCH * POSITIONS // CHUNK
+CHUNK_POOLED = CHUNK // 4
+
+LOAD = 1024
+LOAD_UNITS = BATCH * POSITIONS // LOAD
+CHUNKS_PER_LOAD = LOAD // CHUNK
+LOADS_AHEAD = 2
+
+STORE_CHUNKS = 4
+STORE_POOLED = STORE_CHUNKS * CHUNK_POOLED
+
+VECTOR_POSITIONS = 160
+RUN = 4
+
+FLOPS = 2 * (WEIGHT_TILES * P) * CHANNELS * BATCH * POSITIONS
+
+
+def tile_selfattention_pa_t_kernel(tc, x, Wq, Wk, Wv, out_0, out_1, out_2):
+    nc = tc.nc
+    q_out, k_out, v_out = out_0, out_1, out_2
+
+    with ExitStack() as ctx:
+        ctx.enter_context(tc.manual_schedule())
+        weights = ctx.enter_context(tc.tile_pool(name="weights", bufs=1))
+        raw_pool = ctx.enter_context(tc.tile_pool(name="raw", bufs=PASSES * LOAD_UNITS))
+        stage = ctx.enter_context(tc.tile_pool(name="stage", bufs=3))
+        results = ctx.enter_context(tc.tile_pool(name="results", bufs=2))
+        psum = ctx.enter_context(tc.psum_pool(name="psum", bufs=8))
+
+        identity = weights.tile([P, P], F32, name="identity")
+        make_identity(nc, identity[:])
+
+        weight_rows = (Wq, Wk, Wv[0:P, :], Wv[P : 2 * P, :])
+        w_raw = []
+        for r in range(WEIGHT_TILES):
+            w_raw.append(weights.tile([P, CHANNELS], BF16, name="w_raw_%d" % r))
+            nc.sync.dma_start(out=w_raw[r][:], in_=weight_rows[r])
+
+        raw = {}
+
+        def load_x(unit):
+            b, first = divmod(unit * LOAD, POSITIONS)
+            x_b = x[b].rearrange("k h w -> k (h w)")
+            for c in range(PASSES):
+                raw[(unit, c)] = raw_pool.tile([P, PACK, LOAD], BF16, name="raw")
+                rows = x_b[c * K_PASS : (c + 1) * K_PASS, first : first + LOAD]
+                nc.sync.dma_start(
+                    out=raw[(unit, c)][:], in_=rows.rearrange("(p j) n -> p j n", j=PACK)
+                )
+
+        for unit in range(LOADS_AHEAD):
+            load_x(unit)
+
+        w_grouped = weights.tile(
+            [P, WEIGHT_TILES * PASSES * P * PACK], BF16, name="w_grouped", align_bytes=64
+        )
+        w_grouped_words = w_grouped[:].bitcast(F32)
+        tile_words = PASSES * P * PACK // 2
+        for r in range(WEIGHT_TILES):
+            words = w_raw[r][:].bitcast(F32).rearrange("d (c p u) -> d c u p", c=PASSES, u=2)
+            bank = psum.tile([P, CHUNK], F32, name="bank")
+            turned = bank[:].rearrange("p (c u d) -> p c u d", c=PASSES, u=2)
+            for c in range(PASSES):
+                for u in range(2):
+                    nc.tensor.transpose(turned[:, c, u, :], words[:, c, u, :], identity[:])
+            copy_out = nc.vector.tensor_copy if r % 2 == 0 else nc.scalar.copy
+            copy_out(
+                out=w_grouped_words[:, r * tile_words : (r + 1) * tile_words].rearrange(
+                    "p (c d u) -> p c d u", c=PASSES, u=2
+                ),
+                in_=turned.rearrange("p c u d -> p c d u"),
+            )
+        w_codes = weights.tile([P, WEIGHT_TILES * PASSES * P], U32, name="w_codes", align_bytes=64)
+        w_scales = weights.tile([P, WEIGHT_TILES * PASSES * P], U8, name="w_scales", align_bytes=64)
+        nc.vector.quantize_mx(out=w_codes[:].bitcast(FP8X4), scales=w_scales[:], in_=w_grouped[:])
+
+        def weight_columns(r, c):
+            first = (r * PASSES + c) * P
+            return slice(first, first + P)
+
+        def regroup(i):
+            unit, part = divmod(i, CHUNKS_PER_LOAD)
+            grouped = stage.tile([P, PASSES, CHUNK, PACK], BF16, name="grouped", align_bytes=64)
+            for c in range(PASSES):
+                rows = raw[(unit, c)][:, :, part * CHUNK : (part + 1) * CHUNK]
+                source = rows.rearrange("p j (g i) -> p g j i", i=RUN)
+                target = grouped[:, c, :, :].rearrange("p (g i) j -> p g j i", i=RUN)
+                split = VECTOR_POSITIONS // RUN
+                nc.vector.tensor_copy(out=target[:, :split, :, :], in_=source[:, :split, :, :])
+                nc.scalar.copy(out=target[:, split:, :, :], in_=source[:, split:, :, :])
+            return grouped
+
+        def quantise(grouped):
+            codes = stage.tile([P, PASSES * CHUNK], U32, name="codes", align_bytes=64)
+            scales = stage.tile([P, PASSES * CHUNK], U8, name="scales", align_bytes=64)
+            nc.vector.quantize_mx(
+                out=codes[:].bitcast(FP8X4),
+                scales=scales[:],
+                in_=grouped[:].rearrange("p c n j -> p (c n j)"),
+            )
+            return codes, scales
+
+        def multiply(codes, scales):
+            banks = []
+            for r in range(1, WEIGHT_TILES):
+                bank = psum.tile([P, CHUNK], F32, name="bank")
+                for c in range(PASSES):
+                    x_columns = slice(c * CHUNK, (c + 1) * CHUNK)
+                    nc.tensor.matmul_mx(
+                        out=bank[:],
+                        lhsT=w_codes[:, weight_columns(r, c)].bitcast(FP8X4),
+                        lhsT_scale=w_scales[:, weight_columns(r, c)],
+                        rhs=codes[:, x_columns].bitcast(FP8X4),
+                        rhs_scale=scales[:, x_columns],
+                        start=(c == 0),
+                        stop=(c == PASSES - 1),
+                    )
+                banks.append(bank)
+            q_bank = psum.tile([P, CHUNK], F32, name="bank")
+            for t in range(CHUNK // P):
+                for c in range(PASSES):
+                    x_columns = slice(c * CHUNK + t * P, c * CHUNK + (t + 1) * P)
+                    nc.tensor.matmul_mx(
+                        out=q_bank[:, t * Q_CHANNELS : (t + 1) * Q_CHANNELS],
+                        lhsT=codes[:, x_columns].bitcast(FP8X4),
+                        lhsT_scale=scales[:, x_columns],
+                        rhs=w_codes[:, weight_columns(0, c)].bitcast(FP8X4),
+                        rhs_scale=w_scales[:, weight_columns(0, c)],
+                        start=(c == 0),
+                        stop=(c == PASSES - 1),
+                    )
+            return banks, q_bank
+
+        pooled = {}
+
+        def finish(i, banks, q_bank):
+            b, first = divmod(i * CHUNK, POSITIONS)
+            q_sb = stage.tile([P, CHUNK // P, Q_CHANNELS], F32, name="q_sb")
+            nc.scalar.copy(out=q_sb[:].rearrange("m t d -> m (t d)"), in_=q_bank[:])
+            nc.sync.dma_start(
+                out=q_out[b, first : first + CHUNK, :].rearrange("(t m) d -> m t d", m=P),
+                in_=q_sb[:],
+            )
+            part = i % STORE_CHUNKS
+            if part == 0:
+                for r in range(POOLED_TILES):
+                    pooled[r] = results.tile([P, STORE_POOLED], F32, name="pooled_%d" % r)
+            for r in range(POOLED_TILES):
+                nc.vector.tensor_reduce(
+                    out=pooled[r][:, part * CHUNK_POOLED : (part + 1) * CHUNK_POOLED].rearrange(
+                        "p (hp wp) -> p hp wp", wp=WIDTH // 2
+                    ),
+                    in_=banks[r][:].rearrange(
+                        "p (hp a wp b) -> p hp wp a b", a=2, wp=WIDTH // 2, b=2
+                    ),
+                    axis=mybir.AxisListType.XY,
+                    op=mybir.AluOpType.max,
+                )
+            if part == STORE_CHUNKS - 1:
+                last = (first + CHUNK) // 4
+                columns = slice(last - STORE_POOLED, last)
+                nc.sync.dma_start(out=k_out[b, :, columns], in_=pooled[0][:])
+                nc.sync.dma_start(out=v_out[b, 0:P, columns], in_=pooled[1][:])
+                nc.sync.dma_start(out=v_out[b, P : 2 * P, columns], in_=pooled[2][:])
+
+        grouped_of = {}
+        banks_of = {}
+        for s in range(CHUNKS + 2):
+            if s < CHUNKS:
+                if s % CHUNKS_PER_LOAD == 0 and s // CHUNKS_PER_LOAD + LOADS_AHEAD < LOAD_UNITS:
+                    load_x(s // CHUNKS_PER_LOAD + LOADS_AHEAD)
+                grouped_of[s] = regroup(s)
+            if 1 <= s <= CHUNKS:
+                codes, scales = quantise(grouped_of[s - 1])
+                banks_of[s - 1] = multiply(codes, scales)
+            if s >= 2:
+                banks, q_bank = banks_of[s - 2]
+                finish(s - 2, banks, q_bank)

@@ -25,14 +25,14 @@ CHUNKS = BATCH * POSITIONS // CHUNK
 CHUNK_POOLED = CHUNK // 4
 
 LOAD = 1024
-LOAD_UNITS = BATCH * POSITIONS // LOAD
-CHUNKS_PER_LOAD = LOAD // CHUNK
-LOADS_AHEAD = 2
+CHUNKS_AHEAD = 4
 
 STORE_CHUNKS = 4
 STORE_POOLED = STORE_CHUNKS * CHUNK_POOLED
 
-VECTOR_POSITIONS = 160
+VECTOR_POSITIONS = 96
+SCALAR_POSITIONS = 320
+GPSIMD_POSITIONS = CHUNK - VECTOR_POSITIONS - SCALAR_POSITIONS
 RUN = 4
 
 FLOPS = 2 * (WEIGHT_TILES * P) * CHANNELS * BATCH * POSITIONS
@@ -45,13 +45,36 @@ def tile_selfattention_pa_t_kernel(tc, x, Wq, Wk, Wv, out_0, out_1, out_2):
     with ExitStack() as ctx:
         ctx.enter_context(tc.manual_schedule())
         weights = ctx.enter_context(tc.tile_pool(name="weights", bufs=1))
-        raw_pool = ctx.enter_context(tc.tile_pool(name="raw", bufs=PASSES * LOAD_UNITS))
+        raw_pool = ctx.enter_context(tc.tile_pool(name="raw", bufs=1))
         stage = ctx.enter_context(tc.tile_pool(name="stage", bufs=3))
         results = ctx.enter_context(tc.tile_pool(name="results", bufs=2))
         psum = ctx.enter_context(tc.psum_pool(name="psum", bufs=8))
 
+        load_units = []
+        first = 0
+        while first < BATCH * POSITIONS:
+            load_units.append((first, min(max(first, CHUNK), LOAD)))
+            first += load_units[-1][1]
+
+        raw_of = {}
+
+        def load_x(first, size):
+            b, first_in_b = divmod(first, POSITIONS)
+            x_b = x[b].rearrange("k h w -> k (h w)")
+            raw = raw_pool.tile([P, PASSES, PACK, size], BF16, name="raw_%d" % first)
+            for c in range(PASSES):
+                rows = x_b[c * K_PASS : (c + 1) * K_PASS, first_in_b : first_in_b + size]
+                nc.sync.dma_start(
+                    out=raw[:, c, :, :], in_=rows.rearrange("(p j) n -> p j n", j=PACK)
+                )
+            for part in range(size // CHUNK):
+                raw_of[first // CHUNK + part] = (raw, part * CHUNK)
+
         identity = weights.tile([P, P], F32, name="identity")
         make_identity(nc, identity[:])
+
+        load_x(*load_units[0])
+        units_loaded = 1
 
         weight_rows = (Wq, Wk, Wv[0:P, :], Wv[P : 2 * P, :])
         w_raw = []
@@ -59,58 +82,57 @@ def tile_selfattention_pa_t_kernel(tc, x, Wq, Wk, Wv, out_0, out_1, out_2):
             w_raw.append(weights.tile([P, CHANNELS], BF16, name="w_raw_%d" % r))
             nc.sync.dma_start(out=w_raw[r][:], in_=weight_rows[r])
 
-        raw = {}
-
-        def load_x(unit):
-            b, first = divmod(unit * LOAD, POSITIONS)
-            x_b = x[b].rearrange("k h w -> k (h w)")
-            for c in range(PASSES):
-                raw[(unit, c)] = raw_pool.tile([P, PACK, LOAD], BF16, name="raw")
-                rows = x_b[c * K_PASS : (c + 1) * K_PASS, first : first + LOAD]
-                nc.sync.dma_start(
-                    out=raw[(unit, c)][:], in_=rows.rearrange("(p j) n -> p j n", j=PACK)
-                )
-
-        for unit in range(LOADS_AHEAD):
-            load_x(unit)
-
         w_grouped = weights.tile(
             [P, WEIGHT_TILES * PASSES * P * PACK], BF16, name="w_grouped", align_bytes=64
         )
-        w_grouped_words = w_grouped[:].bitcast(F32)
-        tile_words = PASSES * P * PACK // 2
-        for r in range(WEIGHT_TILES):
-            words = w_raw[r][:].bitcast(F32).rearrange("d (c p u) -> d c u p", c=PASSES, u=2)
-            bank = psum.tile([P, CHUNK], F32, name="bank")
-            turned = bank[:].rearrange("p (c u d) -> p c u d", c=PASSES, u=2)
-            for c in range(PASSES):
-                for u in range(2):
-                    nc.tensor.transpose(turned[:, c, u, :], words[:, c, u, :], identity[:])
-            copy_out = nc.vector.tensor_copy if r % 2 == 0 else nc.scalar.copy
-            copy_out(
-                out=w_grouped_words[:, r * tile_words : (r + 1) * tile_words].rearrange(
-                    "p (c d u) -> p c d u", c=PASSES, u=2
-                ),
-                in_=turned.rearrange("p c u d -> p c d u"),
-            )
         w_codes = weights.tile([P, WEIGHT_TILES * PASSES * P], U32, name="w_codes", align_bytes=64)
         w_scales = weights.tile([P, WEIGHT_TILES * PASSES * P], U8, name="w_scales", align_bytes=64)
-        nc.vector.quantize_mx(out=w_codes[:].bitcast(FP8X4), scales=w_scales[:], in_=w_grouped[:])
+
+        def prepare_weights():
+            w_grouped_words = w_grouped[:].bitcast(F32)
+            tile_words = PASSES * P * PACK // 2
+            for r in range(WEIGHT_TILES):
+                words = w_raw[r][:].bitcast(F32).rearrange("d (c p u) -> d c u p", c=PASSES, u=2)
+                bank = psum.tile([P, CHUNK], F32, name="bank")
+                turned = bank[:].rearrange("p (c u d) -> p c u d", c=PASSES, u=2)
+                for c in range(PASSES):
+                    for u in range(2):
+                        nc.tensor.transpose(turned[:, c, u, :], words[:, c, u, :], identity[:])
+                copy_out = nc.vector.tensor_copy if r % 2 == 0 else nc.scalar.copy
+                copy_out(
+                    out=w_grouped_words[:, r * tile_words : (r + 1) * tile_words].rearrange(
+                        "p (c d u) -> p c d u", c=PASSES, u=2
+                    ),
+                    in_=turned.rearrange("p c u d -> p c d u"),
+                )
+            nc.vector.quantize_mx(
+                out=w_codes[:].bitcast(FP8X4), scales=w_scales[:], in_=w_grouped[:]
+            )
 
         def weight_columns(r, c):
             first = (r * PASSES + c) * P
             return slice(first, first + P)
 
         def regroup(i):
-            unit, part = divmod(i, CHUNKS_PER_LOAD)
+            raw, column = raw_of[i]
             grouped = stage.tile([P, PASSES, CHUNK, PACK], BF16, name="grouped", align_bytes=64)
             for c in range(PASSES):
-                rows = raw[(unit, c)][:, :, part * CHUNK : (part + 1) * CHUNK]
+                rows = raw[:, c, :, column : column + CHUNK]
                 source = rows.rearrange("p j (g i) -> p g j i", i=RUN)
                 target = grouped[:, c, :, :].rearrange("p (g i) j -> p g j i", i=RUN)
-                split = VECTOR_POSITIONS // RUN
-                nc.vector.tensor_copy(out=target[:, :split, :, :], in_=source[:, :split, :, :])
-                nc.scalar.copy(out=target[:, split:, :, :], in_=source[:, split:, :, :])
+                v_end = VECTOR_POSITIONS // RUN
+                s_end = v_end + SCALAR_POSITIONS // RUN
+                nc.vector.tensor_copy(out=target[:, :v_end, :, :], in_=source[:, :v_end, :, :])
+                nc.scalar.copy(out=target[:, v_end:s_end, :, :], in_=source[:, v_end:s_end, :, :])
+            g_first = CHUNK - GPSIMD_POSITIONS
+            nc.gpsimd.tensor_scalar(
+                out=grouped[:, :, g_first:, :],
+                in0=raw[:, :, :, column + g_first : column + CHUNK].rearrange("p c j n -> p c n j"),
+                scalar1=1.0,
+                scalar2=0.0,
+                op0=mybir.AluOpType.mult,
+                op1=mybir.AluOpType.add,
+            )
             return grouped
 
         def quantise(grouped):
@@ -189,10 +211,15 @@ def tile_selfattention_pa_t_kernel(tc, x, Wq, Wk, Wv, out_0, out_1, out_2):
         grouped_of = {}
         banks_of = {}
         for s in range(CHUNKS + 2):
+            while units_loaded < len(load_units) and (
+                load_units[units_loaded][0] < (s + CHUNKS_AHEAD) * CHUNK
+            ):
+                load_x(*load_units[units_loaded])
+                units_loaded += 1
             if s < CHUNKS:
-                if s % CHUNKS_PER_LOAD == 0 and s // CHUNKS_PER_LOAD + LOADS_AHEAD < LOAD_UNITS:
-                    load_x(s // CHUNKS_PER_LOAD + LOADS_AHEAD)
                 grouped_of[s] = regroup(s)
+            if s == 0:
+                prepare_weights()
             if 1 <= s <= CHUNKS:
                 codes, scales = quantise(grouped_of[s - 1])
                 banks_of[s - 1] = multiply(codes, scales)

@@ -25,7 +25,6 @@ CHUNKS = BATCH * POSITIONS // CHUNK
 CHUNK_POOLED = CHUNK // 4
 
 LOAD = 1024
-CHUNKS_AHEAD = 4
 
 STORE_CHUNKS = 4
 STORE_POOLED = STORE_CHUNKS * CHUNK_POOLED
@@ -47,7 +46,7 @@ def tile_selfattention_pa_t_kernel(tc, x, Wq, Wk, Wv, out_0, out_1, out_2):
         weights = ctx.enter_context(tc.tile_pool(name="weights", bufs=1))
         raw_pool = ctx.enter_context(tc.tile_pool(name="raw", bufs=1))
         stage = ctx.enter_context(tc.tile_pool(name="stage", bufs=3))
-        results = ctx.enter_context(tc.tile_pool(name="results", bufs=2))
+        results = ctx.enter_context(tc.tile_pool(name="results", bufs=CHUNKS // STORE_CHUNKS))
         psum = ctx.enter_context(tc.psum_pool(name="psum", bufs=8))
 
         load_units = []
@@ -74,13 +73,15 @@ def tile_selfattention_pa_t_kernel(tc, x, Wq, Wk, Wv, out_0, out_1, out_2):
         make_identity(nc, identity[:])
 
         load_x(*load_units[0])
-        units_loaded = 1
 
         weight_rows = (Wq, Wk, Wv[0:P, :], Wv[P : 2 * P, :])
         w_raw = []
         for r in range(WEIGHT_TILES):
             w_raw.append(weights.tile([P, CHANNELS], BF16, name="w_raw_%d" % r))
             nc.sync.dma_start(out=w_raw[r][:], in_=weight_rows[r])
+
+        for unit in load_units[1:]:
+            load_x(*unit)
 
         w_grouped = weights.tile(
             [P, WEIGHT_TILES * PASSES * P * PACK], BF16, name="w_grouped", align_bytes=64
@@ -182,7 +183,7 @@ def tile_selfattention_pa_t_kernel(tc, x, Wq, Wk, Wv, out_0, out_1, out_2):
             b, first = divmod(i * CHUNK, POSITIONS)
             q_sb = stage.tile([P, CHUNK // P, Q_CHANNELS], F32, name="q_sb")
             nc.scalar.copy(out=q_sb[:].rearrange("m t d -> m (t d)"), in_=q_bank[:])
-            nc.sync.dma_start(
+            nc.gpsimd.dma_start(
                 out=q_out[b, first : first + CHUNK, :].rearrange("(t m) d -> m t d", m=P),
                 in_=q_sb[:],
             )
@@ -211,11 +212,6 @@ def tile_selfattention_pa_t_kernel(tc, x, Wq, Wk, Wv, out_0, out_1, out_2):
         grouped_of = {}
         banks_of = {}
         for s in range(CHUNKS + 2):
-            while units_loaded < len(load_units) and (
-                load_units[units_loaded][0] < (s + CHUNKS_AHEAD) * CHUNK
-            ):
-                load_x(*load_units[units_loaded])
-                units_loaded += 1
             if s < CHUNKS:
                 grouped_of[s] = regroup(s)
             if s == 0:

@@ -25,6 +25,10 @@ CHUNKS = BATCH * POSITIONS // CHUNK
 CHUNK_POOLED = CHUNK // 4
 
 LOAD = 1024
+LOAD_UNITS = BATCH * POSITIONS // LOAD
+CHUNKS_PER_LOAD = LOAD // CHUNK
+CHUNKS_AHEAD = 6
+Q_BUFFERS = 6
 
 STORE_CHUNKS = 4
 STORE_POOLED = STORE_CHUNKS * CHUNK_POOLED
@@ -44,35 +48,14 @@ def tile_selfattention_pa_t_kernel(tc, x, Wq, Wk, Wv, out_0, out_1, out_2):
     with ExitStack() as ctx:
         ctx.enter_context(tc.manual_schedule())
         weights = ctx.enter_context(tc.tile_pool(name="weights", bufs=1))
-        raw_pool = ctx.enter_context(tc.tile_pool(name="raw", bufs=1))
+        raw_pool = ctx.enter_context(tc.tile_pool(name="raw", bufs=LOAD_UNITS))
         stage = ctx.enter_context(tc.tile_pool(name="stage", bufs=3))
+        q_pool = ctx.enter_context(tc.tile_pool(name="q", bufs=Q_BUFFERS))
         results = ctx.enter_context(tc.tile_pool(name="results", bufs=CHUNKS // STORE_CHUNKS))
         psum = ctx.enter_context(tc.psum_pool(name="psum", bufs=8))
 
-        load_units = []
-        first = 0
-        while first < BATCH * POSITIONS:
-            load_units.append((first, min(max(first, CHUNK), LOAD)))
-            first += load_units[-1][1]
-
-        raw_of = {}
-
-        def load_x(first, size):
-            b, first_in_b = divmod(first, POSITIONS)
-            x_b = x[b].rearrange("k h w -> k (h w)")
-            raw = raw_pool.tile([P, PASSES, PACK, size], BF16, name="raw_%d" % first)
-            for c in range(PASSES):
-                rows = x_b[c * K_PASS : (c + 1) * K_PASS, first_in_b : first_in_b + size]
-                nc.sync.dma_start(
-                    out=raw[:, c, :, :], in_=rows.rearrange("(p j) n -> p j n", j=PACK)
-                )
-            for part in range(size // CHUNK):
-                raw_of[first // CHUNK + part] = (raw, part * CHUNK)
-
         identity = weights.tile([P, P], F32, name="identity")
         make_identity(nc, identity[:])
-
-        load_x(*load_units[0])
 
         weight_rows = (Wq, Wk, Wv[0:P, :], Wv[P : 2 * P, :])
         w_raw = []
@@ -80,8 +63,17 @@ def tile_selfattention_pa_t_kernel(tc, x, Wq, Wk, Wv, out_0, out_1, out_2):
             w_raw.append(weights.tile([P, CHANNELS], BF16, name="w_raw_%d" % r))
             nc.sync.dma_start(out=w_raw[r][:], in_=weight_rows[r])
 
-        for unit in load_units[1:]:
-            load_x(*unit)
+        raw_of = {}
+
+        def load_x(unit):
+            b, first = divmod(unit * LOAD, POSITIONS)
+            x_b = x[b].rearrange("k h w -> k (h w)")
+            raw_of[unit] = raw_pool.tile([P, PASSES, PACK, LOAD], BF16, name="raw")
+            for c in range(PASSES):
+                rows = x_b[c * K_PASS : (c + 1) * K_PASS, first : first + LOAD]
+                nc.sync.dma_start(
+                    out=raw_of[unit][:, c, :, :], in_=rows.rearrange("(p j) n -> p j n", j=PACK)
+                )
 
         w_grouped = weights.tile(
             [P, WEIGHT_TILES * PASSES * P * PACK], BF16, name="w_grouped", align_bytes=64
@@ -115,7 +107,8 @@ def tile_selfattention_pa_t_kernel(tc, x, Wq, Wk, Wv, out_0, out_1, out_2):
             return slice(first, first + P)
 
         def regroup(i):
-            raw, column = raw_of[i]
+            unit, part = divmod(i, CHUNKS_PER_LOAD)
+            raw, column = raw_of[unit], part * CHUNK
             grouped = stage.tile([P, PASSES, CHUNK, PACK], BF16, name="grouped", align_bytes=64)
             for c in range(PASSES):
                 rows = raw[:, c, :, column : column + CHUNK]
@@ -147,6 +140,19 @@ def tile_selfattention_pa_t_kernel(tc, x, Wq, Wk, Wv, out_0, out_1, out_2):
             return codes, scales
 
         def multiply(codes, scales):
+            q_bank = psum.tile([P, CHUNK], F32, name="bank")
+            for t in range(CHUNK // P):
+                for c in range(PASSES):
+                    x_columns = slice(c * CHUNK + t * P, c * CHUNK + (t + 1) * P)
+                    nc.tensor.matmul_mx(
+                        out=q_bank[:, t * Q_CHANNELS : (t + 1) * Q_CHANNELS],
+                        lhsT=codes[:, x_columns].bitcast(FP8X4),
+                        lhsT_scale=scales[:, x_columns],
+                        rhs=w_codes[:, weight_columns(0, c)].bitcast(FP8X4),
+                        rhs_scale=w_scales[:, weight_columns(0, c)],
+                        start=(c == 0),
+                        stop=(c == PASSES - 1),
+                    )
             banks = []
             for r in range(1, WEIGHT_TILES):
                 bank = psum.tile([P, CHUNK], F32, name="bank")
@@ -162,28 +168,15 @@ def tile_selfattention_pa_t_kernel(tc, x, Wq, Wk, Wv, out_0, out_1, out_2):
                         stop=(c == PASSES - 1),
                     )
                 banks.append(bank)
-            q_bank = psum.tile([P, CHUNK], F32, name="bank")
-            for t in range(CHUNK // P):
-                for c in range(PASSES):
-                    x_columns = slice(c * CHUNK + t * P, c * CHUNK + (t + 1) * P)
-                    nc.tensor.matmul_mx(
-                        out=q_bank[:, t * Q_CHANNELS : (t + 1) * Q_CHANNELS],
-                        lhsT=codes[:, x_columns].bitcast(FP8X4),
-                        lhsT_scale=scales[:, x_columns],
-                        rhs=w_codes[:, weight_columns(0, c)].bitcast(FP8X4),
-                        rhs_scale=w_scales[:, weight_columns(0, c)],
-                        start=(c == 0),
-                        stop=(c == PASSES - 1),
-                    )
             return banks, q_bank
 
         pooled = {}
 
         def finish(i, banks, q_bank):
             b, first = divmod(i * CHUNK, POSITIONS)
-            q_sb = stage.tile([P, CHUNK // P, Q_CHANNELS], F32, name="q_sb")
+            q_sb = q_pool.tile([P, CHUNK // P, Q_CHANNELS], F32, name="q_sb")
             nc.scalar.copy(out=q_sb[:].rearrange("m t d -> m (t d)"), in_=q_bank[:])
-            nc.gpsimd.dma_start(
+            nc.sync.dma_start(
                 out=q_out[b, first : first + CHUNK, :].rearrange("(t m) d -> m t d", m=P),
                 in_=q_sb[:],
             )
@@ -209,13 +202,16 @@ def tile_selfattention_pa_t_kernel(tc, x, Wq, Wk, Wv, out_0, out_1, out_2):
                 nc.sync.dma_start(out=v_out[b, 0:P, columns], in_=pooled[1][:])
                 nc.sync.dma_start(out=v_out[b, P : 2 * P, columns], in_=pooled[2][:])
 
+        prepare_weights()
+        units_loaded = 0
         grouped_of = {}
         banks_of = {}
         for s in range(CHUNKS + 2):
+            while units_loaded < LOAD_UNITS and units_loaded * CHUNKS_PER_LOAD < s + CHUNKS_AHEAD:
+                load_x(units_loaded)
+                units_loaded += 1
             if s < CHUNKS:
                 grouped_of[s] = regroup(s)
-            if s == 0:
-                prepare_weights()
             if 1 <= s <= CHUNKS:
                 codes, scales = quantise(grouped_of[s - 1])
                 banks_of[s - 1] = multiply(codes, scales)

@@ -33,9 +33,10 @@ Q_BUFFERS = 6
 STORE_CHUNKS = 4
 STORE_POOLED = STORE_CHUNKS * CHUNK_POOLED
 
-VECTOR_POSITIONS = 96
-SCALAR_POSITIONS = 320
-GPSIMD_POSITIONS = CHUNK - VECTOR_POSITIONS - SCALAR_POSITIONS
+SLOTS = PASSES * CHUNK
+TENSOR_SLOTS = 128
+VECTOR_SLOTS = 136
+GPSIMD_SLOTS = 192
 RUN = 4
 
 FLOPS = 2 * (WEIGHT_TILES * P) * CHANNELS * BATCH * POSITIONS
@@ -52,10 +53,13 @@ def tile_selfattention_pa_t_kernel(tc, x, Wq, Wk, Wv, out_0, out_1, out_2):
         stage = ctx.enter_context(tc.tile_pool(name="stage", bufs=3))
         q_pool = ctx.enter_context(tc.tile_pool(name="q", bufs=Q_BUFFERS))
         results = ctx.enter_context(tc.tile_pool(name="results", bufs=CHUNKS // STORE_CHUNKS))
-        psum = ctx.enter_context(tc.psum_pool(name="psum", bufs=8))
+        psum = ctx.enter_context(tc.psum_pool(name="psum", bufs=6))
+        psum_passed = ctx.enter_context(tc.psum_pool(name="psum_passed", bufs=2))
 
         identity = weights.tile([P, P], F32, name="identity")
         make_identity(nc, identity[:])
+        identity_bf = weights.tile([P, P], BF16, name="identity_bf")
+        make_identity(nc, identity_bf[:])
 
         weight_rows = (Wq, Wk, Wv[0:P, :], Wv[P : 2 * P, :])
         w_raw = []
@@ -106,28 +110,65 @@ def tile_selfattention_pa_t_kernel(tc, x, Wq, Wk, Wv, out_0, out_1, out_2):
             first = (r * PASSES + c) * P
             return slice(first, first + P)
 
-        def regroup(i):
+        def raw_columns(i):
             unit, part = divmod(i, CHUNKS_PER_LOAD)
-            raw, column = raw_of[unit], part * CHUNK
-            grouped = stage.tile([P, PASSES, CHUNK, PACK], BF16, name="grouped", align_bytes=64)
-            for c in range(PASSES):
-                rows = raw[:, c, :, column : column + CHUNK]
-                source = rows.rearrange("p j (g i) -> p g j i", i=RUN)
-                target = grouped[:, c, :, :].rearrange("p (g i) j -> p g j i", i=RUN)
-                v_end = VECTOR_POSITIONS // RUN
-                s_end = v_end + SCALAR_POSITIONS // RUN
-                nc.vector.tensor_copy(out=target[:, :v_end, :, :], in_=source[:, :v_end, :, :])
-                nc.scalar.copy(out=target[:, v_end:s_end, :, :], in_=source[:, v_end:s_end, :, :])
-            g_first = CHUNK - GPSIMD_POSITIONS
-            nc.gpsimd.tensor_scalar(
-                out=grouped[:, :, g_first:, :],
-                in0=raw[:, :, :, column + g_first : column + CHUNK].rearrange("p c j n -> p c n j"),
-                scalar1=1.0,
-                scalar2=0.0,
-                op0=mybir.AluOpType.mult,
-                op1=mybir.AluOpType.add,
+            return raw_of[unit], part * CHUNK
+
+        grouped_of = {}
+
+        def pieces(lo, hi, step):
+            cuts = []
+            while lo < hi:
+                end = min(hi, (lo // step + 1) * step)
+                cuts.append((lo // CHUNK, lo % CHUNK, end - lo + lo % CHUNK))
+                lo = end
+            return cuts
+
+        passed_of = {}
+
+        def pass_through(i):
+            raw, column = raw_columns(i)
+            passed = psum_passed.tile([P, TENSOR_SLOTS, PACK], BF16, name="passed")
+            nc.tensor.matmul(
+                out=passed[:],
+                lhsT=identity_bf[:],
+                rhs=raw[:, 0, :, column : column + TENSOR_SLOTS].rearrange("p j n -> p n j"),
+                start=True,
+                stop=True,
             )
-            return grouped
+            passed_of[i] = passed
+
+        def collect(i):
+            grouped_of[i] = stage.tile([P, PASSES, CHUNK, PACK], BF16, name="grouped", align_bytes=64)
+            nc.scalar.copy(
+                out=grouped_of[i][:].rearrange("p c n j -> p (c n j)")[:, : TENSOR_SLOTS * PACK].bitcast(F32),
+                in_=passed_of[i][:].rearrange("p n j -> p (n j)").bitcast(F32),
+            )
+
+        def regroup(i):
+            raw, column = raw_columns(i)
+            grouped = grouped_of[i]
+            shares = (
+                (nc.vector.tensor_copy, TENSOR_SLOTS, TENSOR_SLOTS + VECTOR_SLOTS),
+                (nc.scalar.copy, TENSOR_SLOTS + VECTOR_SLOTS, SLOTS - GPSIMD_SLOTS),
+            )
+            for copy, lo, hi in shares:
+                for c, n0, n1 in pieces(lo, hi, CHUNK):
+                    copy(
+                        out=grouped[:, c, n0:n1, :].rearrange("p (g i) j -> p g j i", i=RUN),
+                        in_=raw[:, c, :, column + n0 : column + n1].rearrange(
+                            "p j (g i) -> p g j i", i=RUN
+                        ),
+                    )
+            for c, n0, n1 in pieces(SLOTS - GPSIMD_SLOTS, SLOTS, CHUNK):
+                nc.gpsimd.tensor_scalar(
+                    out=grouped[:, c, n0:n1, :],
+                    in0=raw[:, c, :, column + n0 : column + n1].rearrange("p j n -> p n j"),
+                    scalar1=1.0,
+                    scalar2=0.0,
+                    op0=mybir.AluOpType.mult,
+                    op1=mybir.AluOpType.add,
+                )
 
         def quantise(grouped):
             codes = stage.tile([P, PASSES * CHUNK], U32, name="codes", align_bytes=64)
@@ -172,7 +213,7 @@ def tile_selfattention_pa_t_kernel(tc, x, Wq, Wk, Wv, out_0, out_1, out_2):
 
         pooled = {}
 
-        def finish(i, banks, q_bank):
+        def finish_q(i, q_bank):
             b, first = divmod(i * CHUNK, POSITIONS)
             q_sb = q_pool.tile([P, CHUNK // P, Q_CHANNELS], F32, name="q_sb")
             nc.scalar.copy(out=q_sb[:].rearrange("m t d -> m (t d)"), in_=q_bank[:])
@@ -180,6 +221,9 @@ def tile_selfattention_pa_t_kernel(tc, x, Wq, Wk, Wv, out_0, out_1, out_2):
                 out=q_out[b, first : first + CHUNK, :].rearrange("(t m) d -> m t d", m=P),
                 in_=q_sb[:],
             )
+
+        def finish_pooled(i, banks):
+            b, first = divmod(i * CHUNK, POSITIONS)
             part = i % STORE_CHUNKS
             if part == 0:
                 for r in range(POOLED_TILES):
@@ -204,17 +248,21 @@ def tile_selfattention_pa_t_kernel(tc, x, Wq, Wk, Wv, out_0, out_1, out_2):
 
         prepare_weights()
         units_loaded = 0
-        grouped_of = {}
         banks_of = {}
-        for s in range(CHUNKS + 2):
+        for s in range(-2, CHUNKS + 2):
             while units_loaded < LOAD_UNITS and units_loaded * CHUNKS_PER_LOAD < s + CHUNKS_AHEAD:
                 load_x(units_loaded)
                 units_loaded += 1
-            if s < CHUNKS:
-                grouped_of[s] = regroup(s)
+            if s + 2 < CHUNKS:
+                pass_through(s + 2)
+            if s >= 2:
+                finish_q(s - 2, banks_of[s - 2][1])
+            if 0 <= s < CHUNKS:
+                regroup(s)
             if 1 <= s <= CHUNKS:
                 codes, scales = quantise(grouped_of[s - 1])
                 banks_of[s - 1] = multiply(codes, scales)
             if s >= 2:
-                banks, q_bank = banks_of[s - 2]
-                finish(s - 2, banks, q_bank)
+                finish_pooled(s - 2, banks_of[s - 2][0])
+            if 0 <= s + 1 < CHUNKS:
+                collect(s + 1)

@@ -34,8 +34,9 @@ STORE_CHUNKS = 4
 STORE_POOLED = STORE_CHUNKS * CHUNK_POOLED
 
 SLOTS = PASSES * CHUNK
-TENSOR_SLOTS = 128
-VECTOR_SLOTS = 136
+TENSOR_SLOTS = 256
+PASS_THROUGH = 128
+VECTOR_SLOTS = 104
 GPSIMD_SLOTS = 192
 RUN = 4
 
@@ -129,13 +130,14 @@ def tile_selfattention_pa_t_kernel(tc, x, Wq, Wk, Wv, out_0, out_1, out_2):
         def pass_through(i):
             raw, column = raw_columns(i)
             passed = psum_passed.tile([P, TENSOR_SLOTS, PACK], BF16, name="passed")
-            nc.tensor.matmul(
-                out=passed[:],
-                lhsT=identity_bf[:],
-                rhs=raw[:, 0, :, column : column + TENSOR_SLOTS].rearrange("p j n -> p n j"),
-                start=True,
-                stop=True,
-            )
+            for n0 in range(0, TENSOR_SLOTS, PASS_THROUGH):
+                nc.tensor.matmul(
+                    out=passed[:, n0 : n0 + PASS_THROUGH, :].rearrange("p n j -> p j n"),
+                    lhsT=identity_bf[:],
+                    rhs=raw[:, 0, :, column + n0 : column + n0 + PASS_THROUGH],
+                    start=True,
+                    stop=True,
+                )
             passed_of[i] = passed
 
         def collect(i):

@@ -34,9 +34,9 @@ STORE_CHUNKS = 4
 STORE_POOLED = STORE_CHUNKS * CHUNK_POOLED
 
 SLOTS = PASSES * CHUNK
-TENSOR_SLOTS = 256
+TENSOR_SLOTS = 192
 PASS_THROUGH = 128
-VECTOR_SLOTS = 104
+VECTOR_SLOTS = 120
 GPSIMD_SLOTS = 192
 RUN = 4
 
@@ -131,10 +131,11 @@ def tile_selfattention_pa_t_kernel(tc, x, Wq, Wk, Wv, out_0, out_1, out_2):
             raw, column = raw_columns(i)
             passed = psum_passed.tile([P, TENSOR_SLOTS, PACK], BF16, name="passed")
             for n0 in range(0, TENSOR_SLOTS, PASS_THROUGH):
+                n1 = min(n0 + PASS_THROUGH, TENSOR_SLOTS)
                 nc.tensor.matmul(
-                    out=passed[:, n0 : n0 + PASS_THROUGH, :].rearrange("p n j -> p j n"),
+                    out=passed[:, n0:n1, :].rearrange("p n j -> p j n"),
                     lhsT=identity_bf[:],
-                    rhs=raw[:, 0, :, column + n0 : column + n0 + PASS_THROUGH],
+                    rhs=raw[:, 0, :, column + n0 : column + n1],
                     start=True,
                     stop=True,
                 )

from contextlib import ExitStack

import concourse.mybir as mybir
from concourse.masks import make_identity

F32 = mybir.dt.float32
BF16 = mybir.dt.bfloat16
U32 = mybir.dt.uint32
U8 = mybir.dt.uint8
FP8X4 = mybir.dt.float8_e4m3fn_x4

P = 128
PACK = 4
K_PASS = P * PACK

BATCH, CHANNELS, HEIGHT, WIDTH = 2, 1024, 64, 64
POSITIONS = HEIGHT * WIDTH
PASSES = CHANNELS // K_PASS
Q_CHANNELS = 128
WEIGHT_TILES = 4
POOLED_TILES = 3

CHUNK = 512
CHUNKS = BATCH * POSITIONS // CHUNK
CHUNK_POOLED = CHUNK // 4

LOAD = 1024
LOAD_UNITS = BATCH * POSITIONS // LOAD
CHUNKS_PER_LOAD = LOAD // CHUNK
CHUNKS_AHEAD = 6
Q_BUFFERS = 6

STORE_CHUNKS = 4
STORE_POOLED = STORE_CHUNKS * CHUNK_POOLED

SLOTS = PASSES * CHUNK
TENSOR_SLOTS = 192
PASS_THROUGH = 128
VECTOR_SLOTS = 120
GPSIMD_SLOTS = 192
RUN = 4

FLOPS = 2 * (WEIGHT_TILES * P) * CHANNELS * BATCH * POSITIONS


def tile_selfattention_pa_t_kernel(tc, x, Wq, Wk, Wv, out_0, out_1, out_2):
    nc = tc.nc
    q_out, k_out, v_out = out_0, out_1, out_2

    with ExitStack() as ctx:
        ctx.enter_context(tc.manual_schedule())
        weights = ctx.enter_context(tc.tile_pool(name="weights", bufs=1))
        raw_pool = ctx.enter_context(tc.tile_pool(name="raw", bufs=LOAD_UNITS))
        stage = ctx.enter_context(tc.tile_pool(name="stage", bufs=3))
        q_pool = ctx.enter_context(tc.tile_pool(name="q", bufs=Q_BUFFERS))
        results = ctx.enter_context(tc.tile_pool(name="results", bufs=CHUNKS // STORE_CHUNKS))
        psum = ctx.enter_context(tc.psum_pool(name="psum", bufs=6))
        psum_passed = ctx.enter_context(tc.psum_pool(name="psum_passed", bufs=2))

        identity = weights.tile([P, P], F32, name="identity")
        make_identity(nc, identity[:])
        identity_bf = weights.tile([P, P], BF16, name="identity_bf")
        make_identity(nc, identity_bf[:])

        weight_rows = (Wq, Wk, Wv[0:P, :], Wv[P : 2 * P, :])
        w_raw = []
        for r in range(WEIGHT_TILES):
            w_raw.append(weights.tile([P, CHANNELS], BF16, name="w_raw_%d" % r))
            nc.sync.dma_start(out=w_raw[r][:], in_=weight_rows[r])

        raw_of = {}

        def load_x(unit):
            b, first = divmod(unit * LOAD, POSITIONS)
            x_b = x[b].rearrange("k h w -> k (h w)")
            raw_of[unit] = raw_pool.tile([P, PASSES, PACK, LOAD], BF16, name="raw")
            for c in range(PASSES):
                rows = x_b[c * K_PASS : (c + 1) * K_PASS, first : first + LOAD]
                nc.sync.dma_start(
                    out=raw_of[unit][:, c, :, :], in_=rows.rearrange("(p j) n -> p j n", j=PACK)
                )

        w_grouped = weights.tile(
            [P, WEIGHT_TILES * PASSES * P * PACK], BF16, name="w_grouped", align_bytes=64
        )
        w_codes = weights.tile([P, WEIGHT_TILES * PASSES * P], U32, name="w_codes", align_bytes=64)
        w_scales = weights.tile([P, WEIGHT_TILES * PASSES * P], U8, name="w_scales", align_bytes=64)

        def prepare_weights():
            w_grouped_words = w_grouped[:].bitcast(F32)
            tile_words = PASSES * P * PACK // 2
            for r in range(WEIGHT_TILES):
                words = w_raw[r][:].bitcast(F32).rearrange("d (c p u) -> d c u p", c=PASSES, u=2)
                bank = psum.tile([P, CHUNK], F32, name="bank")
                turned = bank[:].rearrange("p (c u d) -> p c u d", c=PASSES, u=2)
                for c in range(PASSES):
                    for u in range(2):
                        nc.tensor.transpose(turned[:, c, u, :], words[:, c, u, :], identity[:])
                copy_out = nc.vector.tensor_copy if r % 2 == 0 else nc.scalar.copy
                copy_out(
                    out=w_grouped_words[:, r * tile_words : (r + 1) * tile_words].rearrange(
                        "p (c d u) -> p c d u", c=PASSES, u=2
                    ),
                    in_=turned.rearrange("p c u d -> p c d u"),
                )
            nc.vector.quantize_mx(
                out=w_codes[:].bitcast(FP8X4), scales=w_scales[:], in_=w_grouped[:]
            )

        def weight_columns(r, c):
            first = (r * PASSES + c) * P
            return slice(first, first + P)

        def raw_columns(i):
            unit, part = divmod(i, CHUNKS_PER_LOAD)
            return raw_of[unit], part * CHUNK

        grouped_of = {}

        def pieces(lo, hi, step):
            cuts = []
            while lo < hi:
                end = min(hi, (lo // step + 1) * step)
                cuts.append((lo // CHUNK, lo % CHUNK, end - lo + lo % CHUNK))
                lo = end
            return cuts

        passed_of = {}

        def pass_through(i):
            raw, column = raw_columns(i)
            passed = psum_passed.tile([P, TENSOR_SLOTS, PACK], BF16, name="passed")
            for n0 in range(0, TENSOR_SLOTS, PASS_THROUGH):
                n1 = min(n0 + PASS_THROUGH, TENSOR_SLOTS)
                nc.tensor.matmul(
                    out=passed[:, n0:n1, :].rearrange("p n j -> p j n"),
                    lhsT=identity_bf[:],
                    rhs=raw[:, 0, :, column + n0 : column + n1],
                    start=True,
                    stop=True,
                )
            passed_of[i] = passed

        def collect(i):
            grouped_of[i] = stage.tile([P, PASSES, CHUNK, PACK], BF16, name="grouped", align_bytes=64)
            nc.scalar.copy(
                out=grouped_of[i][:].rearrange("p c n j -> p (c n j)")[:, : TENSOR_SLOTS * PACK].bitcast(F32),
                in_=passed_of[i][:].rearrange("p n j -> p (n j)").bitcast(F32),
            )

        def regroup(i):
            raw, column = raw_columns(i)
            grouped = grouped_of[i]
            shares = (
                (nc.vector.tensor_copy, TENSOR_SLOTS, TENSOR_SLOTS + VECTOR_SLOTS),
                (nc.scalar.copy, TENSOR_SLOTS + VECTOR_SLOTS, SLOTS - GPSIMD_SLOTS),
            )
            for copy, lo, hi in shares:
                for c, n0, n1 in pieces(lo, hi, CHUNK):
                    copy(
                        out=grouped[:, c, n0:n1, :].rearrange("p (g i) j -> p g j i", i=RUN),
                        in_=raw[:, c, :, column + n0 : column + n1].rearrange(
                            "p j (g i) -> p g j i", i=RUN
                        ),
                    )
            for c, n0, n1 in pieces(SLOTS - GPSIMD_SLOTS, SLOTS, CHUNK):
                nc.gpsimd.tensor_scalar(
                    out=grouped[:, c, n0:n1, :],
                    in0=raw[:, c, :, column + n0 : column + n1].rearrange("p j n -> p n j"),
                    scalar1=1.0,
                    scalar2=0.0,
                    op0=mybir.AluOpType.mult,
                    op1=mybir.AluOpType.add,
                )

        def quantise(grouped):
            codes = stage.tile([P, PASSES * CHUNK], U32, name="codes", align_bytes=64)
            scales = stage.tile([P, PASSES * CHUNK], U8, name="scales", align_bytes=64)
            nc.vector.quantize_mx(
                out=codes[:].bitcast(FP8X4),
                scales=scales[:],
                in_=grouped[:].rearrange("p c n j -> p (c n j)"),
            )
            return codes, scales

        def multiply(codes, scales):
            q_bank = psum.tile([P, CHUNK], F32, name="bank")
            for t in range(CHUNK // P):
                for c in range(PASSES):
                    x_columns = slice(c * CHUNK + t * P, c * CHUNK + (t + 1) * P)
                    nc.tensor.matmul_mx(
                        out=q_bank[:, t * Q_CHANNELS : (t + 1) * Q_CHANNELS],
                        lhsT=codes[:, x_columns].bitcast(FP8X4),
                        lhsT_scale=scales[:, x_columns],
                        rhs=w_codes[:, weight_columns(0, c)].bitcast(FP8X4),
                        rhs_scale=w_scales[:, weight_columns(0, c)],
                        start=(c == 0),
                        stop=(c == PASSES - 1),
                    )
            banks = []
            for r in range(1, WEIGHT_TILES):
                bank = psum.tile([P, CHUNK], F32, name="bank")
                for c in range(PASSES):
                    x_columns = slice(c * CHUNK, (c + 1) * CHUNK)
                    nc.tensor.matmul_mx(
                        out=bank[:],
                        lhsT=w_codes[:, weight_columns(r, c)].bitcast(FP8X4),
                        lhsT_scale=w_scales[:, weight_columns(r, c)],
                        rhs=codes[:, x_columns].bitcast(FP8X4),
                        rhs_scale=scales[:, x_columns],
                        start=(c == 0),
                        stop=(c == PASSES - 1),
                    )
                banks.append(bank)
            return banks, q_bank

        pooled = {}

        def finish_q(i, q_bank):
            b, first = divmod(i * CHUNK, POSITIONS)
            q_sb = q_pool.tile([P, CHUNK // P, Q_CHANNELS], F32, name="q_sb")
            nc.scalar.copy(out=q_sb[:].rearrange("m t d -> m (t d)"), in_=q_bank[:])
            nc.sync.dma_start(
                out=q_out[b, first : first + CHUNK, :].rearrange("(t m) d -> m t d", m=P),
                in_=q_sb[:],
            )

        def finish_pooled(i, banks):
            b, first = divmod(i * CHUNK, POSITIONS)
            part = i % STORE_CHUNKS
            if part == 0:
                for r in range(POOLED_TILES):
                    pooled[r] = results.tile([P, STORE_POOLED], F32, name="pooled_%d" % r)
            for r in range(POOLED_TILES):
                nc.vector.tensor_reduce(
                    out=pooled[r][:, part * CHUNK_POOLED : (part + 1) * CHUNK_POOLED].rearrange(
                        "p (hp wp) -> p hp wp", wp=WIDTH // 2
                    ),
                    in_=banks[r][:].rearrange(
                        "p (hp a wp b) -> p hp wp a b", a=2, wp=WIDTH // 2, b=2
                    ),
                    axis=mybir.AxisListType.XY,
                    op=mybir.AluOpType.max,
                )
            if part == STORE_CHUNKS - 1:
                last = (first + CHUNK) // 4
                columns = slice(last - STORE_POOLED, last)
                nc.sync.dma_start(out=k_out[b, :, columns], in_=pooled[0][:])
                nc.sync.dma_start(out=v_out[b, 0:P, columns], in_=pooled[1][:])
                nc.sync.dma_start(out=v_out[b, P : 2 * P, columns], in_=pooled[2][:])

        prepare_weights()
        units_loaded = 0
        banks_of = {}
        for s in range(-2, CHUNKS + 2):
            while units_loaded < LOAD_UNITS and units_loaded * CHUNKS_PER_LOAD < s + CHUNKS_AHEAD:
                load_x(units_loaded)
                units_loaded += 1
            if s + 2 < CHUNKS:
                pass_through(s + 2)
            if s >= 2:
                finish_q(s - 2, banks_of[s - 2][1])
            if 0 <= s < CHUNKS:
                regroup(s)
            if 1 <= s <= CHUNKS:
                codes, scales = quantise(grouped_of[s - 1])
                banks_of[s - 1] = multiply(codes, scales)
            if s >= 2:
                finish_pooled(s - 2, banks_of[s - 2][0])
            if 0 <= s + 1 < CHUNKS:
                collect(s + 1)
